import numpy as np
import ml_dtypes


def mxq(x, axis, fmt="e4m3"):
    dtype, down = {"e4m3": (ml_dtypes.float8_e4m3fn, 7), "e5m2": (ml_dtypes.float8_e5m2, 14)}[fmt]
    v = np.moveaxis(np.asarray(x, np.float32).astype(ml_dtypes.bfloat16).astype(np.float64), axis, -1)
    blocks = v.reshape(v.shape[:-1] + (-1, 32))
    amax = np.abs(blocks).max(-1, keepdims=True)
    byte = np.maximum(np.where(amax > 0, np.frexp(amax)[1] - 1 + 127, 0) - down, 1)
    scale = np.exp2(byte - 127.0)
    codes = (blocks / scale).astype(np.float32).astype(dtype).astype(np.float64)
    return np.moveaxis((codes * scale).reshape(v.shape), -1, axis)


WIDE = False


def mx_kscale(k):
    if not WIDE:
        return np.ones(k)
    levels = np.array([10, -10, 5, -5, 0])
    if k % 512:
        return np.exp2(np.random.permutation(np.resize(levels, k // 32))).repeat(32)
    a = np.empty((k // 512, 16))
    for p in range(k // 512):
        a[p, :8] = np.random.permutation(np.resize(levels, 8))
        for g in range(8):
            far = levels[np.abs(levels - a[p, g]) >= 10]
            a[p, g + 8] = far[np.random.randint(len(far))]
    return np.exp2(a.ravel()).repeat(32)


BF16 = ml_dtypes.bfloat16


def bf(x):
    return np.asarray(x, np.float32).astype(BF16)


def f64(x):
    return np.asarray(x).astype(np.float64)


B, S, D, F = 4, 1024, 512, 1024
EPS = 1e-6


def setup_inputs():
    s = mx_kscale(D)
    p = np.exp2(np.round(np.log2(np.mean(1.0 / s**2)) / 2))
    q = np.exp2(np.round(np.log2(np.mean(s**2)) / 2))
    return {"x": bf(np.random.standard_normal((B, S, D)) * 0.5 * s * p),
            "weight": bf(np.random.standard_normal((F, D)) * 0.5 / s * q),
            "alpha": bf(1.0 + 0.1 * np.random.standard_normal(1)),
            "bias": bf(0.1 * np.random.standard_normal(F))}


def reference(x, weight, alpha, bias):
    x = f64(x)
    weight = f64(weight)
    nf = weight.shape[0]
    y = mxq(x, 2, "e4m3") @ mxq(weight, 1, "e4m3").T
    x_sq = np.sum(x * x, axis=-1, keepdims=True)
    w_sq = np.sum(weight * weight, axis=-1)
    distances = x_sq + w_sq - 2.0 * y
    out = (y * y) / (distances + EPS)
    scale = (np.sqrt(nf) / np.log(1.0 + nf)) ** f64(alpha)
    out = out * scale + f64(bias)
    return out

@@ -1,0 +1,321 @@
+import math
+from contextlib import ExitStack
+
+import concourse.mybir as mybir
+from concourse.masks import make_identity
+
+F32 = mybir.dt.float32
+BF16 = mybir.dt.bfloat16
+U32 = mybir.dt.uint32
+U8 = mybir.dt.uint8
+FP8X4 = mybir.dt.float8_e4m3fn_x4
+ALU = mybir.AluOpType
+ACT = mybir.ActivationFunctionType
+
+P = 128
+PACK = 4
+TOKENS = 4096
+K = 512
+FEATS = 1024
+TOKEN_TILES = TOKENS // P
+FEAT_TILES = FEATS // P
+PAIRS = TOKEN_TILES // 2
+BANK = 512
+HALVES = FEATS // BANK
+GROUP = 4
+EPS = 1e-6
+ROOT_OF_BASE = math.sqrt(math.sqrt(FEATS) / math.log(1.0 + FEATS))
+
+FLOPS = 2 * TOKENS * K * FEATS
+
+FIRST_STEP = -2
+VECTOR_TAIL = 2
+GRAM_PAIRS = range(3, 14)
+VECTOR_COPIES = (12, 14)
+BIAS_BANK_STEP = 26
+
+
+def turn_step(m):
+    return m // 2 - 4
+
+
+def turn_bank(m):
+    return m - 2 if m < 6 else 4 + m % 2
+
+
+def quantise_step(g):
+    return g - 2
+
+
+def gram_step(m):
+    return max(m + 1, 2 * m - 4)
+
+
+def square_step(j):
+    return j - 3 if j < 6 else 2 * (j - 23)
+
+
+def product_bank(k, h):
+    return (6, 0, 2)[k % 3] + h
+
+
+def tile_yatdense_t_kernel(tc, x, weight, alpha, bias, out):
+    nc = tc.nc
+    x_view = x.flatten_outer_dims().rearrange("(p j) k -> p (j k)", j=TOKEN_TILES)
+    out_view = out.flatten_outer_dims().rearrange("(p j) n -> p j n", j=TOKEN_TILES)
+    w_view = weight.rearrange("(i p) k -> p i k", p=P)
+
+    with ExitStack() as ctx:
+        keep = ctx.enter_context(tc.tile_pool(name="keep", bufs=1))
+        stage = ctx.enter_context(tc.tile_pool(name="stage", bufs=3))
+        work = ctx.enter_context(tc.tile_pool(name="work", bufs=3))
+        store = ctx.enter_context(tc.tile_pool(name="store", bufs=4))
+        psum = ctx.enter_context(tc.psum_pool(name="psum", bufs=1))
+        ctx.enter_context(tc.manual_schedule())
+
+        def bank(n):
+            return psum.tile([P, BANK], F32, name="bank%d" % n)
+
+        w_sb = keep.tile([P, FEAT_TILES * K], BF16)
+        x_sb = keep.tile([P, TOKEN_TILES * K], BF16)
+        alpha_bf = keep.tile([P, 1], BF16)
+        bias_bf = keep.tile([P, FEATS], BF16)
+
+        def load_x(first, last):
+            nc.sync.dma_start(out=x_sb[:, first * K : last * K], in_=x_view[:, first * K : last * K])
+
+        for first, last in ((0, 2), (2, 4), (4, 8)):
+            nc.sync.dma_start(
+                out=w_sb[:, first * K : last * K].rearrange("p (i k) -> p i k", k=K), in_=w_view[:, first:last, :]
+            )
+        load_x(0, 4)
+        nc.sync.dma_start(out=alpha_bf[:], in_=alpha.partition_broadcast(P))
+        load_x(4, 8)
+        load_x(8, 16)
+        load_x(16, 24)
+        load_x(24, 32)
+        nc.sync.dma_start(out=bias_bf[:], in_=bias.partition_broadcast(P))
+
+        ident = keep.tile([P, P], F32)
+        make_identity(nc, ident[:])
+        ident_bf = keep.tile([P, P], BF16)
+        make_identity(nc, ident_bf[:])
+
+        one = keep.tile([P, 1], F32)
+        nc.vector.memset(one[:], 1.0)
+        warm = keep.tile([P, 1], F32)
+        nc.scalar.activation(out=warm[:], in_=one[:], func=ACT.Abs_reciprocal_sqrt)
+
+        w_t = keep.tile([P, FEAT_TILES * K], BF16, align_bytes=64)
+        x_t = keep.tile([P, TOKEN_TILES * K], BF16, align_bytes=64)
+        w_codes = keep.tile([P, FEATS], U32, align_bytes=64)
+        w_scales = keep.tile([P, FEATS], U8, align_bytes=64)
+        x_codes = keep.tile([P, TOKENS], U32, align_bytes=64)
+        x_scales = keep.tile([P, TOKENS], U8, align_bytes=64)
+        w_sq = keep.tile([P, FEAT_TILES], F32)
+        x_sq = keep.tile([P, TOKEN_TILES], F32)
+        x_sq_gram = keep.tile([P, TOKEN_TILES], F32)
+        w_sq_rows = keep.tile([P, FEATS], F32)
+        sigma = keep.tile([P, 1], F32)
+        halves = [slice(h * BANK, (h + 1) * BANK) for h in range(HALVES)]
+
+        turned = {}
+
+        def turn(name, src, m, n):
+            turned[name, m] = bank(n)
+            view = turned[name, m][:].rearrange("p (j u r) -> p j u r", j=2, u=2)
+            words = src[:].bitcast(F32)
+            for jj in range(2):
+                for u in range(2):
+                    c0 = (2 * m + jj) * (K // 2)
+                    nc.tensor.transpose(view[:, jj, u, :], words[:, c0 + u : c0 + K // 2 : 2], ident[:])
+
+        def regroup(name, dst, m, on_scalar):
+            to = dst[:].bitcast(F32).rearrange("p (j r u) -> p j r u", r=P, u=2)[:, 2 * m : 2 * m + 2, :, :]
+            src = turned[name, m][:].rearrange("p (j u r) -> p j r u", j=2, u=2)
+            if on_scalar:
+                nc.scalar.copy(out=to, in_=src)
+            else:
+                nc.vector.tensor_copy(out=to, in_=src)
+
+        def quantise(src, codes, scales, g):
+            cols = slice(g * GROUP * P, (g + 1) * GROUP * P)
+            nc.vector.quantize_mx(
+                out=codes[:, cols].bitcast(FP8X4),
+                scales=scales[:, cols],
+                in_=src[:, g * GROUP * K : (g + 1) * GROUP * K],
+            )
+
+        def square_sum(src, j, dst):
+            junk = stage.tile([P, K], BF16, name="junk")
+            nc.scalar.activation(out=junk[:], in_=src[:, j * K : (j + 1) * K], func=ACT.Square, accum_out=dst[:, j : j + 1])
+
+        y = {}
+        e = {}
+        q = {}
+        t = {}
+        sq = {}
+        o = {}
+        gram = {}
+        bias_bank = []
+
+        def multiply(k):
+            rows = slice(k * P, (k + 1) * P)
+            y[k] = []
+            for h in range(HALVES):
+                product = bank(product_bank(k, h))
+                nc.tensor.matmul_mx(
+                    out=product[:],
+                    lhsT=x_codes[:, rows].bitcast(FP8X4),
+                    lhsT_scale=x_scales[:, rows],
+                    rhs=w_codes[:, halves[h]].bitcast(FP8X4),
+                    rhs_scale=w_scales[:, halves[h]],
+                    start=True,
+                    stop=True,
+                )
+                y[k].append(product)
+
+        def gram_products(m):
+            gram[m] = bank(4 + m % 2)
+            view = x_t[:].rearrange("p (j r t) -> p j r t", r=P, t=PACK)
+            for jj in range(2):
+                for tt in range(PACK):
+                    operand = view[:, 2 * m + jj, :, tt]
+                    nc.tensor.matmul(
+                        out=gram[m][:, jj * P : (jj + 1) * P], lhsT=operand, rhs=operand,
+                        start=(tt == 0), stop=(tt == PACK - 1),
+                    )
+
+        def gram_diagonals(m):
+            for jj in range(2):
+                masked = stage.tile([P, P], F32, name="masked")
+                nc.vector.scalar_tensor_tensor(
+                    out=masked[:], in0=gram[m][:, jj * P : (jj + 1) * P], scalar=1.0, in1=ident[:],
+                    op0=ALU.mult, op1=ALU.mult, accum_out=x_sq_gram[:, 2 * m + jj : 2 * m + jj + 1],
+                )
+
+        def stage_a(k):
+            e[k] = work.tile([P, FEATS], F32, name="e")
+            for h in range(HALVES):
+                nc.vector.scalar_tensor_tensor(
+                    out=e[k][:, halves[h]], in0=y[k][h][:], scalar=-2.0, in1=w_sq_rows[:, halves[h]],
+                    op0=ALU.mult, op1=ALU.add,
+                )
+
+        def stage_b(k):
+            q[k] = work.tile([P, FEATS], F32, name="q")
+            nc.scalar.activation(
+                out=q[k][:], in_=e[k][:], func=ACT.Abs_reciprocal_sqrt,
+                bias=(x_sq_gram if k // 2 in GRAM_PAIRS else x_sq)[:, k : k + 1], scale=1.0,
+            )
+
+        def stage_c(k):
+            t[k] = work.tile([P, FEATS], F32, name="t")
+            for h in range(HALVES):
+                nc.vector.tensor_tensor(out=t[k][:, halves[h]], in0=y[k][h][:], in1=q[k][:, halves[h]], op=ALU.mult)
+
+        def stage_d(k):
+            sq[k] = work.tile([P, FEATS], F32, name="sq")
+            nc.scalar.activation(out=sq[k][:], in_=t[k][:], func=ACT.Square, scale=sigma[:, 0:1])
+
+        def stage_e(k):
+            o[k] = store.tile([P, FEATS], F32, name="o")
+            nc.gpsimd.tensor_tensor(out=o[k][:], in0=sq[k][:], in1=bias_bf[:], op=ALU.add)
+
+        def store_tile(k):
+            nc.sync.dma_start(out=out_view[:, k, :], in_=o[k][:])
+
+        def stage_e_vector(k):
+            o[k] = store.tile([P, FEATS], F32, name="o")
+            for h in range(HALVES):
+                nc.vector.tensor_tensor(out=o[k][:, halves[h]], in0=sq[k][:, halves[h]], in1=bias_bank[h][:], op=ALU.add)
+                nc.sync.dma_start(out=out_view[:, k, halves[h]], in_=o[k][:, halves[h]])
+
+        turn("w", w_sb, 0, 0)
+        turn("w", w_sb, 1, 1)
+        for i in range(4):
+            square_sum(w_sb, i, w_sq)
+        regroup("w", w_t, 0, False)
+        regroup("w", w_t, 1, False)
+        turn("w", w_sb, 2, 2)
+        turn("w", w_sb, 3, 3)
+        for i in range(4, FEAT_TILES):
+            square_sum(w_sb, i, w_sq)
+        quantise(w_t, w_codes, w_scales, 0)
+        regroup("w", w_t, 2, False)
+        regroup("w", w_t, 3, False)
+        turn("x", x_sb, 0, 4)
+        turn("x", x_sb, 1, 5)
+        regroup("x", x_t, 0, False)
+        quantise(w_t, w_codes, w_scales, 1)
+        regroup("x", x_t, 1, False)
+        turn("x", x_sb, 2, 6)
+        turn("x", x_sb, 3, 7)
+        spread = [bank(0), bank(1)]
+        for i in range(FEAT_TILES):
+            nc.tensor.transpose(
+                spread[i // 4][:, (i % 4) * P : (i % 4 + 1) * P], w_sq[:, i : i + 1].to_broadcast([P, P]), ident[:]
+            )
+        square_sum(x_sb, 0, x_sq)
+        regroup("x", x_t, 2, True)
+        regroup("x", x_t, 3, True)
+        quantise(x_t, x_codes, x_scales, 0)
+        for h in range(HALVES):
+            nc.vector.tensor_scalar_add(out=w_sq_rows[:, halves[h]], in0=spread[h][:], scalar1=EPS)
+
+        alpha_f = keep.tile([P, 1], F32)
+        nc.gpsimd.tensor_copy(out=alpha_f[:], in_=alpha_bf[:])
+        root = keep.tile([P, 1], F32)
+        nc.gpsimd.tensor_scalar(
+            out=root[:], in0=alpha_f[:], scalar1=0.0, scalar2=ROOT_OF_BASE, op0=ALU.mult, op1=ALU.add
+        )
+        nc.gpsimd.tensor_tensor(out=sigma[:], in0=root[:], in1=alpha_f[:], op=ALU.pow)
+
+        last = TOKEN_TILES - 1
+        for i in range(FIRST_STEP, last):
+            if i + 2 <= last:
+                multiply(i + 2)
+            for m in range(4, PAIRS):
+                if turn_step(m) == i:
+                    turn("x", x_sb, m, turn_bank(m))
+            for m in GRAM_PAIRS:
+                if gram_step(m) == i:
+                    gram_products(m)
+            if i == BIAS_BANK_STEP:
+                for h in range(HALVES):
+                    bias_bank.append(bank(4 + h))
+                    nc.tensor.matmul(out=bias_bank[h][:], lhsT=ident_bf[:], rhs=bias_bf[:, halves[h]], start=True, stop=True)
+            for m in GRAM_PAIRS:
+                if gram_step(m) + 1 == i:
+                    gram_diagonals(m)
+            for g in range(1, TOKEN_TILES // GROUP):
+                if quantise_step(g) == i:
+                    quantise(x_t, x_codes, x_scales, g)
+            if i >= 0:
+                stage_c(i)
+            for m in VECTOR_COPIES:
+                if turn_step(m) == i:
+                    regroup("x", x_t, m, False)
+            if i + 2 <= last:
+                stage_a(i + 2)
+            if i >= 1:
+                stage_d(i - 1)
+            if i >= -1:
+                stage_b(i + 1)
+            for j in range(1, TOKEN_TILES):
+                if j // 2 not in GRAM_PAIRS and square_step(j) == i:
+                    square_sum(x_sb, j, x_sq)
+            for m in range(4, PAIRS):
+                if turn_step(m) == i and m not in VECTOR_COPIES:
+                    regroup("x", x_t, m, True)
+            if i >= 2:
+                stage_e(i - 2)
+                store_tile(i - 2)
+
+        stage_c(last)
+        stage_d(last - 1)
+        stage_e(last - 2)
+        stage_d(last)
+        stage_e_vector(last - 1)
+        store_tile(last - 2)
+        stage_e_vector(last)

@@ -31,20 +31,21 @@ FLOPS = 2 * TOKENS * K * FEATS
 FIRST_STEP = -2
 VECTOR_TAIL = 2
 GRAM_PAIRS = range(3, 14)
-VECTOR_COPIES = (12, 14)
+HEAD_PAIRS = 8
+VECTOR_COPIES = (11, 15)
 BIAS_BANK_STEP = 26
 
 
 def turn_step(m):
-    return m // 2 - 4
+    return FIRST_STEP + (m - HEAD_PAIRS) // 4
 
 
 def turn_bank(m):
-    return m - 2 if m < 6 else 4 + m % 2
+    return 4 + m if m < 4 else 2 + m % 4
 
 
 def quantise_step(g):
-    return g - 2
+    return FIRST_STEP + (g - 1) // 2
 
 
 def gram_step(m):
@@ -52,7 +53,7 @@ def gram_step(m):
 
 
 def square_step(j):
-    return j - 3 if j < 6 else 2 * (j - 23)
+    return j - 2 if j < 6 else 2 * (j - 23)
 
 
 def product_bank(k, h):
@@ -251,14 +252,22 @@ def tile_yatdense_t_kernel(tc, x, weight, alpha, bias, out):
         regroup("x", x_t, 1, False)
         turn("x", x_sb, 2, 6)
         turn("x", x_sb, 3, 7)
+        turn("x", x_sb, 4, turn_bank(4))
+        turn("x", x_sb, 5, turn_bank(5))
         spread = [bank(0), bank(1)]
         for i in range(FEAT_TILES):
             nc.tensor.transpose(
                 spread[i // 4][:, (i % 4) * P : (i % 4 + 1) * P], w_sq[:, i : i + 1].to_broadcast([P, P]), ident[:]
             )
-        square_sum(x_sb, 0, x_sq)
+        turn("x", x_sb, 6, turn_bank(6))
+        turn("x", x_sb, 7, turn_bank(7))
         regroup("x", x_t, 2, True)
         regroup("x", x_t, 3, True)
+        regroup("x", x_t, 4, True)
+        regroup("x", x_t, 5, True)
+        square_sum(x_sb, 0, x_sq)
+        regroup("x", x_t, 6, True)
+        regroup("x", x_t, 7, True)
         quantise(x_t, x_codes, x_scales, 0)
         for h in range(HALVES):
             nc.vector.tensor_scalar_add(out=w_sq_rows[:, halves[h]], in0=spread[h][:], scalar1=EPS)
@@ -275,7 +284,7 @@ def tile_yatdense_t_kernel(tc, x, weight, alpha, bias, out):
         for i in range(FIRST_STEP, last):
             if i + 2 <= last:
                 multiply(i + 2)
-            for m in range(4, PAIRS):
+            for m in range(HEAD_PAIRS, PAIRS):
                 if turn_step(m) == i:
                     turn("x", x_sb, m, turn_bank(m))
             for m in GRAM_PAIRS:
@@ -305,7 +314,7 @@ def tile_yatdense_t_kernel(tc, x, weight, alpha, bias, out):
             for j in range(1, TOKEN_TILES):
                 if j // 2 not in GRAM_PAIRS and square_step(j) == i:
                     square_sum(x_sb, j, x_sq)
-            for m in range(4, PAIRS):
+            for m in range(HEAD_PAIRS, PAIRS):
                 if turn_step(m) == i and m not in VECTOR_COPIES:
                     regroup("x", x_t, m, True)
             if i >= 2:

@@ -31,8 +31,8 @@ FLOPS = 2 * TOKENS * K * FEATS
 FIRST_STEP = -2
 VECTOR_TAIL = 2
 GRAM_PAIRS = range(3, 14)
-HEAD_PAIRS = 8
-VECTOR_COPIES = (11, 15)
+HEAD_PAIRS = 6
+VECTOR_COPIES = (11, 15,)
 BIAS_BANK_STEP = 26
 
 
@@ -45,11 +45,11 @@ def turn_bank(m):
 
 
 def quantise_step(g):
-    return FIRST_STEP + (g - 1) // 2
+    return max(FIRST_STEP, turn_step(2 * g + 1) + 1)
 
 
 def gram_step(m):
-    return max(m + 1, 2 * m - 4)
+    return max(m, 2 * m - 4)
 
 
 def square_step(j):
@@ -252,22 +252,18 @@ def tile_yatdense_t_kernel(tc, x, weight, alpha, bias, out):
         regroup("x", x_t, 1, False)
         turn("x", x_sb, 2, 6)
         turn("x", x_sb, 3, 7)
-        turn("x", x_sb, 4, turn_bank(4))
-        turn("x", x_sb, 5, turn_bank(5))
         spread = [bank(0), bank(1)]
         for i in range(FEAT_TILES):
             nc.tensor.transpose(
                 spread[i // 4][:, (i % 4) * P : (i % 4 + 1) * P], w_sq[:, i : i + 1].to_broadcast([P, P]), ident[:]
             )
-        turn("x", x_sb, 6, turn_bank(6))
-        turn("x", x_sb, 7, turn_bank(7))
+        turn("x", x_sb, 4, turn_bank(4))
+        turn("x", x_sb, 5, turn_bank(5))
         regroup("x", x_t, 2, True)
         regroup("x", x_t, 3, True)
         regroup("x", x_t, 4, True)
         regroup("x", x_t, 5, True)
         square_sum(x_sb, 0, x_sq)
-        regroup("x", x_t, 6, True)
-        regroup("x", x_t, 7, True)
         quantise(x_t, x_codes, x_scales, 0)
         for h in range(HALVES):
             nc.vector.tensor_scalar_add(out=w_sq_rows[:, halves[h]], in0=spread[h][:], scalar1=EPS)
@@ -294,19 +290,6 @@ def tile_yatdense_t_kernel(tc, x, weight, alpha, bias, out):
                 for h in range(HALVES):
                     bias_bank.append(bank(4 + h))
                     nc.tensor.matmul(out=bias_bank[h][:], lhsT=ident_bf[:], rhs=bias_bf[:, halves[h]], start=True, stop=True)
-            for m in GRAM_PAIRS:
-                if gram_step(m) + 1 == i:
-                    gram_diagonals(m)
-            for g in range(1, TOKEN_TILES // GROUP):
-                if quantise_step(g) == i:
-                    quantise(x_t, x_codes, x_scales, g)
-            if i >= 0:
-                stage_c(i)
-            for m in VECTOR_COPIES:
-                if turn_step(m) == i:
-                    regroup("x", x_t, m, False)
-            if i + 2 <= last:
-                stage_a(i + 2)
             if i >= 1:
                 stage_d(i - 1)
             if i >= -1:
@@ -317,6 +300,19 @@ def tile_yatdense_t_kernel(tc, x, weight, alpha, bias, out):
             for m in range(HEAD_PAIRS, PAIRS):
                 if turn_step(m) == i and m not in VECTOR_COPIES:
                     regroup("x", x_t, m, True)
+            if i >= 0:
+                stage_c(i)
+            if i + 2 <= last:
+                stage_a(i + 2)
+            for m in VECTOR_COPIES:
+                if turn_step(m) == i:
+                    regroup("x", x_t, m, False)
+            for g in range(1, TOKEN_TILES // GROUP):
+                if quantise_step(g) == i:
+                    quantise(x_t, x_codes, x_scales, g)
+            for m in GRAM_PAIRS:
+                if gram_step(m) + 1 == i:
+                    gram_diagonals(m)
             if i >= 2:
                 stage_e(i - 2)
                 store_tile(i - 2)

@@ -223,14 +223,34 @@ def tile_yatdense_t_kernel(tc, x, weight, alpha, bias, out):
             o[k] = store.tile([P, FEATS], F32, name="o")
             nc.gpsimd.tensor_tensor(out=o[k][:], in0=sq[k][:], in1=bias_bf[:], op=ALU.add)
 
+        def stage_b_half(k, h):
+            if h == 0:
+                q[k] = work.tile([P, FEATS], F32, name="q")
+            nc.scalar.activation(
+                out=q[k][:, halves[h]], in_=e[k][:, halves[h]], func=ACT.Abs_reciprocal_sqrt,
+                bias=(x_sq_gram if k // 2 in GRAM_PAIRS else x_sq)[:, k : k + 1], scale=1.0,
+            )
+
+        def stage_d_half(k, h):
+            if h == 0:
+                sq[k] = work.tile([P, FEATS], F32, name="sq")
+            nc.scalar.activation(out=sq[k][:, halves[h]], in_=t[k][:, halves[h]], func=ACT.Square, scale=sigma[:, 0:1])
+
         def store_tile(k):
             nc.sync.dma_start(out=out_view[:, k, :], in_=o[k][:])
 
-        def stage_e_vector(k):
-            o[k] = store.tile([P, FEATS], F32, name="o")
-            for h in range(HALVES):
+        def stage_e_half(k, h, on_vector):
+            if h == 0:
+                o[k] = store.tile([P, FEATS], F32, name="o")
+            if on_vector:
                 nc.vector.tensor_tensor(out=o[k][:, halves[h]], in0=sq[k][:, halves[h]], in1=bias_bank[h][:], op=ALU.add)
-                nc.sync.dma_start(out=out_view[:, k, halves[h]], in_=o[k][:, halves[h]])
+            else:
+                nc.gpsimd.tensor_tensor(out=o[k][:, halves[h]], in0=sq[k][:, halves[h]], in1=bias_bf[:, halves[h]], op=ALU.add)
+            nc.sync.dma_start(out=out_view[:, k, halves[h]], in_=o[k][:, halves[h]])
+
+        warm_bank = bank(7)
+        for i in range(5):
+            nc.tensor.transpose(warm_bank[:, 0:P], ident[:], ident[:])
 
         turn("w", w_sb, 0, 0)
         turn("w", w_sb, 1, 1)
@@ -261,12 +281,12 @@ def tile_yatdense_t_kernel(tc, x, weight, alpha, bias, out):
         turn("x", x_sb, 5, turn_bank(5))
         regroup("x", x_t, 2, True)
         regroup("x", x_t, 3, True)
+        nc.scalar.activation(out=w_sq_rows[:, halves[0]], in_=spread[0][:], func=ACT.Identity, bias=EPS)
         regroup("x", x_t, 4, True)
         regroup("x", x_t, 5, True)
         square_sum(x_sb, 0, x_sq)
         quantise(x_t, x_codes, x_scales, 0)
-        for h in range(HALVES):
-            nc.vector.tensor_scalar_add(out=w_sq_rows[:, halves[h]], in0=spread[h][:], scalar1=EPS)
+        nc.vector.tensor_scalar_add(out=w_sq_rows[:, halves[1]], in0=spread[1][:], scalar1=EPS)
 
         alpha_f = keep.tile([P, 1], F32)
         nc.gpsimd.tensor_copy(out=alpha_f[:], in_=alpha_bf[:])
@@ -292,8 +312,11 @@ def tile_yatdense_t_kernel(tc, x, weight, alpha, bias, out):
                     nc.tensor.matmul(out=bias_bank[h][:], lhsT=ident_bf[:], rhs=bias_bf[:, halves[h]], start=True, stop=True)
             if i >= 1:
                 stage_d(i - 1)
-            if i >= -1:
+            if -1 <= i < last - 1:
                 stage_b(i + 1)
+            if i == last - 1:
+                stage_b_half(last, 0)
+                stage_b_half(last, 1)
             for j in range(1, TOKEN_TILES):
                 if j // 2 not in GRAM_PAIRS and square_step(j) == i:
                     square_sum(x_sb, j, x_sq)
@@ -319,8 +342,11 @@ def tile_yatdense_t_kernel(tc, x, weight, alpha, bias, out):
 
         stage_c(last)
         stage_d(last - 1)
-        stage_e(last - 2)
-        stage_d(last)
-        stage_e_vector(last - 1)
-        store_tile(last - 2)
-        stage_e_vector(last)
+        stage_e_half(last - 2, 0, False)
+        stage_e_half(last - 2, 1, False)
+        stage_d_half(last, 0)
+        stage_d_half(last, 1)
+        stage_e_half(last - 1, 0, True)
+        stage_e_half(last, 0, True)
+        stage_e_half(last, 1, True)
+        stage_e_half(last - 1, 1, False)

@@ -70,6 +70,7 @@ def tile_yatdense_t_kernel(tc, x, weight, alpha, bias, out):
         keep = ctx.enter_context(tc.tile_pool(name="keep", bufs=1))
         stage = ctx.enter_context(tc.tile_pool(name="stage", bufs=3))
         work = ctx.enter_context(tc.tile_pool(name="work", bufs=3))
+        deep = ctx.enter_context(tc.tile_pool(name="deep", bufs=6))
         store = ctx.enter_context(tc.tile_pool(name="store", bufs=4))
         psum = ctx.enter_context(tc.psum_pool(name="psum", bufs=1))
         ctx.enter_context(tc.manual_schedule())
@@ -216,7 +217,7 @@ def tile_yatdense_t_kernel(tc, x, weight, alpha, bias, out):
                 nc.vector.tensor_tensor(out=t[k][:, halves[h]], in0=y[k][h][:], in1=q[k][:, halves[h]], op=ALU.mult)
 
         def stage_d(k):
-            sq[k] = work.tile([P, FEATS], F32, name="sq")
+            sq[k] = deep.tile([P, FEATS], F32, name="sq")
             nc.scalar.activation(out=sq[k][:], in_=t[k][:], func=ACT.Square, scale=sigma[:, 0:1])
 
         def stage_e(k):
@@ -233,19 +234,16 @@ def tile_yatdense_t_kernel(tc, x, weight, alpha, bias, out):
 
         def stage_d_half(k, h):
             if h == 0:
-                sq[k] = work.tile([P, FEATS], F32, name="sq")
+                sq[k] = deep.tile([P, FEATS], F32, name="sq")
             nc.scalar.activation(out=sq[k][:, halves[h]], in_=t[k][:, halves[h]], func=ACT.Square, scale=sigma[:, 0:1])
 
         def store_tile(k):
             nc.sync.dma_start(out=out_view[:, k, :], in_=o[k][:])
 
-        def stage_e_half(k, h, on_vector):
+        def stage_e_half(k, h):
             if h == 0:
                 o[k] = store.tile([P, FEATS], F32, name="o")
-            if on_vector:
-                nc.vector.tensor_tensor(out=o[k][:, halves[h]], in0=sq[k][:, halves[h]], in1=bias_bank[h][:], op=ALU.add)
-            else:
-                nc.gpsimd.tensor_tensor(out=o[k][:, halves[h]], in0=sq[k][:, halves[h]], in1=bias_bf[:, halves[h]], op=ALU.add)
+            nc.vector.tensor_tensor(out=o[k][:, halves[h]], in0=sq[k][:, halves[h]], in1=bias_bank[h][:], op=ALU.add)
             nc.sync.dma_start(out=out_view[:, k, halves[h]], in_=o[k][:, halves[h]])
 
         warm_bank = bank(7)
@@ -342,11 +340,8 @@ def tile_yatdense_t_kernel(tc, x, weight, alpha, bias, out):
 
         stage_c(last)
         stage_d(last - 1)
-        stage_e_half(last - 2, 0, False)
-        stage_e_half(last - 2, 1, False)
         stage_d_half(last, 0)
         stage_d_half(last, 1)
-        stage_e_half(last - 1, 0, True)
-        stage_e_half(last, 0, True)
-        stage_e_half(last, 1, True)
-        stage_e_half(last - 1, 1, False)
+        for k in range(last - 2, last + 1):
+            for h in range(HALVES):
+                stage_e_half(k, h)

@@ -30,7 +30,7 @@ FLOPS = 2 * TOKENS * K * FEATS
 
 FIRST_STEP = -2
 VECTOR_TAIL = 2
-GRAM_PAIRS = range(3, 14)
+GRAM_TILES = range(6, 28)
 HEAD_PAIRS = 6
 VECTOR_COPIES = (11, 15,)
 BIAS_BANK_STEP = 26
@@ -48,8 +48,8 @@ def quantise_step(g):
     return max(FIRST_STEP, turn_step(2 * g + 1) + 1)
 
 
-def gram_step(m):
-    return max(m, 2 * m - 4)
+def gram_step(j):
+    return j - 4
 
 
 def square_step(j):
@@ -177,24 +177,19 @@ def tile_yatdense_t_kernel(tc, x, weight, alpha, bias, out):
                 )
                 y[k].append(product)
 
-        def gram_products(m):
-            gram[m] = bank(4 + m % 2)
+        def gram_product(j):
+            gram[j] = bank(4 + j % 2)
             view = x_t[:].rearrange("p (j r t) -> p j r t", r=P, t=PACK)
-            for jj in range(2):
-                for tt in range(PACK):
-                    operand = view[:, 2 * m + jj, :, tt]
-                    nc.tensor.matmul(
-                        out=gram[m][:, jj * P : (jj + 1) * P], lhsT=operand, rhs=operand,
-                        start=(tt == 0), stop=(tt == PACK - 1),
-                    )
+            for tt in range(PACK):
+                operand = view[:, j, :, tt]
+                nc.tensor.matmul(out=gram[j][:, 0:P], lhsT=operand, rhs=operand, start=(tt == 0), stop=(tt == PACK - 1))
 
-        def gram_diagonals(m):
-            for jj in range(2):
-                masked = stage.tile([P, P], F32, name="masked")
-                nc.vector.scalar_tensor_tensor(
-                    out=masked[:], in0=gram[m][:, jj * P : (jj + 1) * P], scalar=1.0, in1=ident[:],
-                    op0=ALU.mult, op1=ALU.mult, accum_out=x_sq_gram[:, 2 * m + jj : 2 * m + jj + 1],
-                )
+        def gram_diagonal(j):
+            masked = stage.tile([P, P], F32, name="masked")
+            nc.vector.scalar_tensor_tensor(
+                out=masked[:], in0=gram[j][:, 0:P], scalar=1.0, in1=ident[:],
+                op0=ALU.mult, op1=ALU.mult, accum_out=x_sq_gram[:, j : j + 1],
+            )
 
         def stage_a(k):
             e[k] = work.tile([P, FEATS], F32, name="e")
@@ -208,7 +203,7 @@ def tile_yatdense_t_kernel(tc, x, weight, alpha, bias, out):
             q[k] = work.tile([P, FEATS], F32, name="q")
             nc.scalar.activation(
                 out=q[k][:], in_=e[k][:], func=ACT.Abs_reciprocal_sqrt,
-                bias=(x_sq_gram if k // 2 in GRAM_PAIRS else x_sq)[:, k : k + 1], scale=1.0,
+                bias=(x_sq_gram if k in GRAM_TILES else x_sq)[:, k : k + 1], scale=1.0,
             )
 
         def stage_c(k):
@@ -229,7 +224,7 @@ def tile_yatdense_t_kernel(tc, x, weight, alpha, bias, out):
                 q[k] = work.tile([P, FEATS], F32, name="q")
             nc.scalar.activation(
                 out=q[k][:, halves[h]], in_=e[k][:, halves[h]], func=ACT.Abs_reciprocal_sqrt,
-                bias=(x_sq_gram if k // 2 in GRAM_PAIRS else x_sq)[:, k : k + 1], scale=1.0,
+                bias=(x_sq_gram if k in GRAM_TILES else x_sq)[:, k : k + 1], scale=1.0,
             )
 
         def stage_d_half(k, h):
@@ -301,9 +296,9 @@ def tile_yatdense_t_kernel(tc, x, weight, alpha, bias, out):
             for m in range(HEAD_PAIRS, PAIRS):
                 if turn_step(m) == i:
                     turn("x", x_sb, m, turn_bank(m))
-            for m in GRAM_PAIRS:
-                if gram_step(m) == i:
-                    gram_products(m)
+            for j in GRAM_TILES:
+                if gram_step(j) == i:
+                    gram_product(j)
             if i == BIAS_BANK_STEP:
                 for h in range(HALVES):
                     bias_bank.append(bank(4 + h))
@@ -316,7 +311,7 @@ def tile_yatdense_t_kernel(tc, x, weight, alpha, bias, out):
                 stage_b_half(last, 0)
                 stage_b_half(last, 1)
             for j in range(1, TOKEN_TILES):
-                if j // 2 not in GRAM_PAIRS and square_step(j) == i:
+                if j not in GRAM_TILES and square_step(j) == i:
                     square_sum(x_sb, j, x_sq)
             for m in range(HEAD_PAIRS, PAIRS):
                 if turn_step(m) == i and m not in VECTOR_COPIES:
@@ -331,9 +326,9 @@ def tile_yatdense_t_kernel(tc, x, weight, alpha, bias, out):
             for g in range(1, TOKEN_TILES // GROUP):
                 if quantise_step(g) == i:
                     quantise(x_t, x_codes, x_scales, g)
-            for m in GRAM_PAIRS:
-                if gram_step(m) + 1 == i:
-                    gram_diagonals(m)
+            for j in GRAM_TILES:
+                if gram_step(j) + 1 == i:
+                    gram_diagonal(j)
             if i >= 2:
                 stage_e(i - 2)
                 store_tile(i - 2)

@@ -91,11 +91,11 @@ def tile_yatdense_t_kernel(tc, x, weight, alpha, bias, out):
                 out=w_sb[:, first * K : last * K].rearrange("p (i k) -> p i k", k=K), in_=w_view[:, first:last, :]
             )
         load_x(0, 4)
-        nc.sync.dma_start(out=alpha_bf[:], in_=alpha.partition_broadcast(P))
         load_x(4, 8)
         load_x(8, 16)
         load_x(16, 24)
         load_x(24, 32)
+        nc.sync.dma_start(out=alpha_bf[:], in_=alpha.partition_broadcast(P))
         nc.sync.dma_start(out=bias_bf[:], in_=bias.partition_broadcast(P))
 
         ident = keep.tile([P, P], F32)

@@ -70,8 +70,8 @@ def tile_yatdense_t_kernel(tc, x, weight, alpha, bias, out):
         keep = ctx.enter_context(tc.tile_pool(name="keep", bufs=1))
         stage = ctx.enter_context(tc.tile_pool(name="stage", bufs=3))
         work = ctx.enter_context(tc.tile_pool(name="work", bufs=3))
-        deep = ctx.enter_context(tc.tile_pool(name="deep", bufs=6))
-        store = ctx.enter_context(tc.tile_pool(name="store", bufs=4))
+        deep = ctx.enter_context(tc.tile_pool(name="deep", bufs=3))
+        store = ctx.enter_context(tc.tile_pool(name="store", bufs=3))
         psum = ctx.enter_context(tc.psum_pool(name="psum", bufs=1))
         ctx.enter_context(tc.manual_schedule())
 
@@ -193,11 +193,18 @@ def tile_yatdense_t_kernel(tc, x, weight, alpha, bias, out):
 
         def stage_a(k):
             e[k] = work.tile([P, FEATS], F32, name="e")
-            for h in range(HALVES):
+            for h in reversed(range(HALVES)):
                 nc.vector.scalar_tensor_tensor(
                     out=e[k][:, halves[h]], in0=y[k][h][:], scalar=-2.0, in1=w_sq_rows[:, halves[h]],
                     op0=ALU.mult, op1=ALU.add,
                 )
+
+        pair_tiles = {}
+
+        def half_of_pair(pool, name, k):
+            if k % 2 == 0:
+                pair_tiles[name] = pool.tile([P, 2 * FEATS], F32, name=name)
+            return pair_tiles[name][:, (k % 2) * FEATS : (k % 2 + 1) * FEATS]
 
         def stage_b(k):
             q[k] = work.tile([P, FEATS], F32, name="q")
@@ -212,11 +219,11 @@ def tile_yatdense_t_kernel(tc, x, weight, alpha, bias, out):
                 nc.vector.tensor_tensor(out=t[k][:, halves[h]], in0=y[k][h][:], in1=q[k][:, halves[h]], op=ALU.mult)
 
         def stage_d(k):
-            sq[k] = deep.tile([P, FEATS], F32, name="sq")
+            sq[k] = half_of_pair(deep, "sq", k)
             nc.scalar.activation(out=sq[k][:], in_=t[k][:], func=ACT.Square, scale=sigma[:, 0:1])
 
         def stage_e(k):
-            o[k] = store.tile([P, FEATS], F32, name="o")
+            o[k] = half_of_pair(store, "o", k)
             nc.gpsimd.tensor_tensor(out=o[k][:], in0=sq[k][:], in1=bias_bf[:], op=ALU.add)
 
         def stage_b_half(k, h):
@@ -229,7 +236,7 @@ def tile_yatdense_t_kernel(tc, x, weight, alpha, bias, out):
 
         def stage_d_half(k, h):
             if h == 0:
-                sq[k] = deep.tile([P, FEATS], F32, name="sq")
+                sq[k] = half_of_pair(deep, "sq", k)
             nc.scalar.activation(out=sq[k][:, halves[h]], in_=t[k][:, halves[h]], func=ACT.Square, scale=sigma[:, 0:1])
 
         def store_tile(k):
@@ -237,7 +244,7 @@ def tile_yatdense_t_kernel(tc, x, weight, alpha, bias, out):
 
         def stage_e_half(k, h):
             if h == 0:
-                o[k] = store.tile([P, FEATS], F32, name="o")
+                o[k] = half_of_pair(store, "o", k)
             nc.vector.tensor_tensor(out=o[k][:, halves[h]], in0=sq[k][:, halves[h]], in1=bias_bank[h][:], op=ALU.add)
             nc.sync.dma_start(out=out_view[:, k, halves[h]], in_=o[k][:, halves[h]])
 

@@ -30,7 +30,7 @@ FLOPS = 2 * TOKENS * K * FEATS
 
 FIRST_STEP = -2
 VECTOR_TAIL = 2
-GRAM_TILES = range(6, 28)
+GRAM_TILES = range(6, 26)
 HEAD_PAIRS = 6
 VECTOR_COPIES = (11, 15,)
 BIAS_BANK_STEP = 26
@@ -92,7 +92,8 @@ def tile_yatdense_t_kernel(tc, x, weight, alpha, bias, out):
             )
         load_x(0, 4)
         load_x(4, 8)
-        load_x(8, 16)
+        load_x(8, 12)
+        load_x(12, 16)
         load_x(16, 24)
         load_x(24, 32)
         nc.sync.dma_start(out=alpha_bf[:], in_=alpha.partition_broadcast(P))
@@ -140,12 +141,12 @@ def tile_yatdense_t_kernel(tc, x, weight, alpha, bias, out):
             else:
                 nc.vector.tensor_copy(out=to, in_=src)
 
-        def quantise(src, codes, scales, g):
-            cols = slice(g * GROUP * P, (g + 1) * GROUP * P)
+        def quantise(src, codes, scales, g, groups=1):
+            cols = slice(g * GROUP * P, (g + groups) * GROUP * P)
             nc.vector.quantize_mx(
                 out=codes[:, cols].bitcast(FP8X4),
                 scales=scales[:, cols],
-                in_=src[:, g * GROUP * K : (g + 1) * GROUP * K],
+                in_=src[:, g * GROUP * K : (g + groups) * GROUP * K],
             )
 
         def square_sum(src, j, dst):
@@ -330,9 +331,9 @@ def tile_yatdense_t_kernel(tc, x, weight, alpha, bias, out):
             for m in VECTOR_COPIES:
                 if turn_step(m) == i:
                     regroup("x", x_t, m, False)
-            for g in range(1, TOKEN_TILES // GROUP):
+            for g in (1, 3, 5, 7):
                 if quantise_step(g) == i:
-                    quantise(x_t, x_codes, x_scales, g)
+                    quantise(x_t, x_codes, x_scales, g, 1 if g == 7 else 2)
             for j in GRAM_TILES:
                 if gram_step(j) + 1 == i:
                     gram_diagonal(j)

import math
from contextlib import ExitStack

import concourse.mybir as mybir
from concourse.masks import make_identity

F32 = mybir.dt.float32
BF16 = mybir.dt.bfloat16
U32 = mybir.dt.uint32
U8 = mybir.dt.uint8
FP8X4 = mybir.dt.float8_e4m3fn_x4
ALU = mybir.AluOpType
ACT = mybir.ActivationFunctionType

P = 128
PACK = 4
TOKENS = 4096
K = 512
FEATS = 1024
TOKEN_TILES = TOKENS // P
FEAT_TILES = FEATS // P
PAIRS = TOKEN_TILES // 2
BANK = 512
HALVES = FEATS // BANK
GROUP = 4
EPS = 1e-6
ROOT_OF_BASE = math.sqrt(math.sqrt(FEATS) / math.log(1.0 + FEATS))

FLOPS = 2 * TOKENS * K * FEATS

FIRST_STEP = -2
VECTOR_TAIL = 2
GRAM_TILES = range(6, 26)
HEAD_PAIRS = 6
VECTOR_COPIES = (11, 15,)
BIAS_BANK_STEP = 26


def turn_step(m):
    return FIRST_STEP + (m - HEAD_PAIRS) // 4


def turn_bank(m):
    return 4 + m if m < 4 else 2 + m % 4


def quantise_step(g):
    return max(FIRST_STEP, turn_step(2 * g + 1) + 1)


def gram_step(j):
    return j - 4


def square_step(j):
    return j - 2 if j < 6 else 2 * (j - 23)


def product_bank(k, h):
    return (6, 0, 2)[k % 3] + h


def tile_yatdense_t_kernel(tc, x, weight, alpha, bias, out):
    nc = tc.nc
    x_view = x.flatten_outer_dims().rearrange("(p j) k -> p (j k)", j=TOKEN_TILES)
    out_view = out.flatten_outer_dims().rearrange("(p j) n -> p j n", j=TOKEN_TILES)
    w_view = weight.rearrange("(i p) k -> p i k", p=P)

    with ExitStack() as ctx:
        keep = ctx.enter_context(tc.tile_pool(name="keep", bufs=1))
        stage = ctx.enter_context(tc.tile_pool(name="stage", bufs=3))
        work = ctx.enter_context(tc.tile_pool(name="work", bufs=3))
        deep = ctx.enter_context(tc.tile_pool(name="deep", bufs=3))
        store = ctx.enter_context(tc.tile_pool(name="store", bufs=3))
        psum = ctx.enter_context(tc.psum_pool(name="psum", bufs=1))
        ctx.enter_context(tc.manual_schedule())

        def bank(n):
            return psum.tile([P, BANK], F32, name="bank%d" % n)

        w_sb = keep.tile([P, FEAT_TILES * K], BF16)
        x_sb = keep.tile([P, TOKEN_TILES * K], BF16)
        alpha_bf = keep.tile([P, 1], BF16)
        bias_bf = keep.tile([P, FEATS], BF16)

        def load_x(first, last):
            nc.sync.dma_start(out=x_sb[:, first * K : last * K], in_=x_view[:, first * K : last * K])

        for first, last in ((0, 2), (2, 4), (4, 8)):
            nc.sync.dma_start(
                out=w_sb[:, first * K : last * K].rearrange("p (i k) -> p i k", k=K), in_=w_view[:, first:last, :]
            )
        load_x(0, 4)
        load_x(4, 8)
        load_x(8, 12)
        load_x(12, 16)
        load_x(16, 24)
        load_x(24, 32)
        nc.sync.dma_start(out=alpha_bf[:], in_=alpha.partition_broadcast(P))
        nc.sync.dma_start(out=bias_bf[:], in_=bias.partition_broadcast(P))

        ident = keep.tile([P, P], F32)
        make_identity(nc, ident[:])
        ident_bf = keep.tile([P, P], BF16)
        make_identity(nc, ident_bf[:])

        one = keep.tile([P, 1], F32)
        nc.vector.memset(one[:], 1.0)
        warm = keep.tile([P, 1], F32)
        nc.scalar.activation(out=warm[:], in_=one[:], func=ACT.Abs_reciprocal_sqrt)

        w_t = keep.tile([P, FEAT_TILES * K], BF16, align_bytes=64)
        x_t = keep.tile([P, TOKEN_TILES * K], BF16, align_bytes=64)
        w_codes = keep.tile([P, FEATS], U32, align_bytes=64)
        w_scales = keep.tile([P, FEATS], U8, align_bytes=64)
        x_codes = keep.tile([P, TOKENS], U32, align_bytes=64)
        x_scales = keep.tile([P, TOKENS], U8, align_bytes=64)
        w_sq = keep.tile([P, FEAT_TILES], F32)
        x_sq = keep.tile([P, TOKEN_TILES], F32)
        x_sq_gram = keep.tile([P, TOKEN_TILES], F32)
        w_sq_rows = keep.tile([P, FEATS], F32)
        sigma = keep.tile([P, 1], F32)
        halves = [slice(h * BANK, (h + 1) * BANK) for h in range(HALVES)]

        turned = {}

        def turn(name, src, m, n):
            turned[name, m] = bank(n)
            view = turned[name, m][:].rearrange("p (j u r) -> p j u r", j=2, u=2)
            words = src[:].bitcast(F32)
            for jj in range(2):
                for u in range(2):
                    c0 = (2 * m + jj) * (K // 2)
                    nc.tensor.transpose(view[:, jj, u, :], words[:, c0 + u : c0 + K // 2 : 2], ident[:])

        def regroup(name, dst, m, on_scalar):
            to = dst[:].bitcast(F32).rearrange("p (j r u) -> p j r u", r=P, u=2)[:, 2 * m : 2 * m + 2, :, :]
            src = turned[name, m][:].rearrange("p (j u r) -> p j r u", j=2, u=2)
            if on_scalar:
                nc.scalar.copy(out=to, in_=src)
            else:
                nc.vector.tensor_copy(out=to, in_=src)

        def quantise(src, codes, scales, g, groups=1):
            cols = slice(g * GROUP * P, (g + groups) * GROUP * P)
            nc.vector.quantize_mx(
                out=codes[:, cols].bitcast(FP8X4),
                scales=scales[:, cols],
                in_=src[:, g * GROUP * K : (g + groups) * GROUP * K],
            )

        def square_sum(src, j, dst):
            junk = stage.tile([P, K], BF16, name="junk")
            nc.scalar.activation(out=junk[:], in_=src[:, j * K : (j + 1) * K], func=ACT.Square, accum_out=dst[:, j : j + 1])

        y = {}
        e = {}
        q = {}
        t = {}
        sq = {}
        o = {}
        gram = {}
        bias_bank = []

        def multiply(k):
            rows = slice(k * P, (k + 1) * P)
            y[k] = []
            for h in range(HALVES):
                product = bank(product_bank(k, h))
                nc.tensor.matmul_mx(
                    out=product[:],
                    lhsT=x_codes[:, rows].bitcast(FP8X4),
                    lhsT_scale=x_scales[:, rows],
                    rhs=w_codes[:, halves[h]].bitcast(FP8X4),
                    rhs_scale=w_scales[:, halves[h]],
                    start=True,
                    stop=True,
                )
                y[k].append(product)

        def gram_product(j):
            gram[j] = bank(4 + j % 2)
            view = x_t[:].rearrange("p (j r t) -> p j r t", r=P, t=PACK)
            for tt in range(PACK):
                operand = view[:, j, :, tt]
                nc.tensor.matmul(out=gram[j][:, 0:P], lhsT=operand, rhs=operand, start=(tt == 0), stop=(tt == PACK - 1))

        def gram_diagonal(j):
            masked = stage.tile([P, P], F32, name="masked")
            nc.vector.scalar_tensor_tensor(
                out=masked[:], in0=gram[j][:, 0:P], scalar=1.0, in1=ident[:],
                op0=ALU.mult, op1=ALU.mult, accum_out=x_sq_gram[:, j : j + 1],
            )

        def stage_a(k):
            e[k] = work.tile([P, FEATS], F32, name="e")
            for h in reversed(range(HALVES)):
                nc.vector.scalar_tensor_tensor(
                    out=e[k][:, halves[h]], in0=y[k][h][:], scalar=-2.0, in1=w_sq_rows[:, halves[h]],
                    op0=ALU.mult, op1=ALU.add,
                )

        pair_tiles = {}

        def half_of_pair(pool, name, k):
            if k % 2 == 0:
                pair_tiles[name] = pool.tile([P, 2 * FEATS], F32, name=name)
            return pair_tiles[name][:, (k % 2) * FEATS : (k % 2 + 1) * FEATS]

        def stage_b(k):
            q[k] = work.tile([P, FEATS], F32, name="q")
            nc.scalar.activation(
                out=q[k][:], in_=e[k][:], func=ACT.Abs_reciprocal_sqrt,
                bias=(x_sq_gram if k in GRAM_TILES else x_sq)[:, k : k + 1], scale=1.0,
            )

        def stage_c(k):
            t[k] = work.tile([P, FEATS], F32, name="t")
            for h in range(HALVES):
                nc.vector.tensor_tensor(out=t[k][:, halves[h]], in0=y[k][h][:], in1=q[k][:, halves[h]], op=ALU.mult)

        def stage_d(k):
            sq[k] = half_of_pair(deep, "sq", k)
            nc.scalar.activation(out=sq[k][:], in_=t[k][:], func=ACT.Square, scale=sigma[:, 0:1])

        def stage_e(k):
            o[k] = half_of_pair(store, "o", k)
            nc.gpsimd.tensor_tensor(out=o[k][:], in0=sq[k][:], in1=bias_bf[:], op=ALU.add)

        def stage_b_half(k, h):
            if h == 0:
                q[k] = work.tile([P, FEATS], F32, name="q")
            nc.scalar.activation(
                out=q[k][:, halves[h]], in_=e[k][:, halves[h]], func=ACT.Abs_reciprocal_sqrt,
                bias=(x_sq_gram if k in GRAM_TILES else x_sq)[:, k : k + 1], scale=1.0,
            )

        def stage_d_half(k, h):
            if h == 0:
                sq[k] = half_of_pair(deep, "sq", k)
            nc.scalar.activation(out=sq[k][:, halves[h]], in_=t[k][:, halves[h]], func=ACT.Square, scale=sigma[:, 0:1])

        def store_tile(k):
            nc.sync.dma_start(out=out_view[:, k, :], in_=o[k][:])

        def stage_e_half(k, h):
            if h == 0:
                o[k] = half_of_pair(store, "o", k)
            nc.vector.tensor_tensor(out=o[k][:, halves[h]], in0=sq[k][:, halves[h]], in1=bias_bank[h][:], op=ALU.add)
            nc.sync.dma_start(out=out_view[:, k, halves[h]], in_=o[k][:, halves[h]])

        warm_bank = bank(7)
        for i in range(5):
            nc.tensor.transpose(warm_bank[:, 0:P], ident[:], ident[:])

        turn("w", w_sb, 0, 0)
        turn("w", w_sb, 1, 1)
        for i in range(4):
            square_sum(w_sb, i, w_sq)
        regroup("w", w_t, 0, False)
        regroup("w", w_t, 1, False)
        turn("w", w_sb, 2, 2)
        turn("w", w_sb, 3, 3)
        for i in range(4, FEAT_TILES):
            square_sum(w_sb, i, w_sq)
        quantise(w_t, w_codes, w_scales, 0)
        regroup("w", w_t, 2, False)
        regroup("w", w_t, 3, False)
        turn("x", x_sb, 0, 4)
        turn("x", x_sb, 1, 5)
        regroup("x", x_t, 0, False)
        quantise(w_t, w_codes, w_scales, 1)
        regroup("x", x_t, 1, False)
        turn("x", x_sb, 2, 6)
        turn("x", x_sb, 3, 7)
        spread = [bank(0), bank(1)]
        for i in range(FEAT_TILES):
            nc.tensor.transpose(
                spread[i // 4][:, (i % 4) * P : (i % 4 + 1) * P], w_sq[:, i : i + 1].to_broadcast([P, P]), ident[:]
            )
        turn("x", x_sb, 4, turn_bank(4))
        turn("x", x_sb, 5, turn_bank(5))
        regroup("x", x_t, 2, True)
        regroup("x", x_t, 3, True)
        nc.scalar.activation(out=w_sq_rows[:, halves[0]], in_=spread[0][:], func=ACT.Identity, bias=EPS)
        regroup("x", x_t, 4, True)
        regroup("x", x_t, 5, True)
        square_sum(x_sb, 0, x_sq)
        quantise(x_t, x_codes, x_scales, 0)
        nc.vector.tensor_scalar_add(out=w_sq_rows[:, halves[1]], in0=spread[1][:], scalar1=EPS)

        alpha_f = keep.tile([P, 1], F32)
        nc.gpsimd.tensor_copy(out=alpha_f[:], in_=alpha_bf[:])
        root = keep.tile([P, 1], F32)
        nc.gpsimd.tensor_scalar(
            out=root[:], in0=alpha_f[:], scalar1=0.0, scalar2=ROOT_OF_BASE, op0=ALU.mult, op1=ALU.add
        )
        nc.gpsimd.tensor_tensor(out=sigma[:], in0=root[:], in1=alpha_f[:], op=ALU.pow)

        last = TOKEN_TILES - 1
        for i in range(FIRST_STEP, last):
            if i + 2 <= last:
                multiply(i + 2)
            for m in range(HEAD_PAIRS, PAIRS):
                if turn_step(m) == i:
                    turn("x", x_sb, m, turn_bank(m))
            for j in GRAM_TILES:
                if gram_step(j) == i:
                    gram_product(j)
            if i == BIAS_BANK_STEP:
                for h in range(HALVES):
                    bias_bank.append(bank(4 + h))
                    nc.tensor.matmul(out=bias_bank[h][:], lhsT=ident_bf[:], rhs=bias_bf[:, halves[h]], start=True, stop=True)
            if i >= 1:
                stage_d(i - 1)
            if -1 <= i < last - 1:
                stage_b(i + 1)
            if i == last - 1:
                stage_b_half(last, 0)
                stage_b_half(last, 1)
            for j in range(1, TOKEN_TILES):
                if j not in GRAM_TILES and square_step(j) == i:
                    square_sum(x_sb, j, x_sq)
            for m in range(HEAD_PAIRS, PAIRS):
                if turn_step(m) == i and m not in VECTOR_COPIES:
                    regroup("x", x_t, m, True)
            if i >= 0:
                stage_c(i)
            if i + 2 <= last:
                stage_a(i + 2)
            for m in VECTOR_COPIES:
                if turn_step(m) == i:
                    regroup("x", x_t, m, False)
            for g in (1, 3, 5, 7):
                if quantise_step(g) == i:
                    quantise(x_t, x_codes, x_scales, g, 1 if g == 7 else 2)
            for j in GRAM_TILES:
                if gram_step(j) + 1 == i:
                    gram_diagonal(j)
            if i >= 2:
                stage_e(i - 2)
                store_tile(i - 2)

        stage_c(last)
        stage_d(last - 1)
        stage_d_half(last, 0)
        stage_d_half(last, 1)
        for k in range(last - 2, last + 1):
            for h in range(HALVES):
                stage_e_half(k, h)
